import numpy as np
import ml_dtypes


def mxq(x, axis, fmt="e4m3"):
    dtype, down = {"e4m3": (ml_dtypes.float8_e4m3fn, 7), "e5m2": (ml_dtypes.float8_e5m2, 14)}[fmt]
    v = np.moveaxis(np.asarray(x, np.float32).astype(ml_dtypes.bfloat16).astype(np.float64), axis, -1)
    blocks = v.reshape(v.shape[:-1] + (-1, 32))
    amax = np.abs(blocks).max(-1, keepdims=True)
    byte = np.maximum(np.where(amax > 0, np.frexp(amax)[1] - 1 + 127, 0) - down, 1)
    scale = np.exp2(byte - 127.0)
    codes = (blocks / scale).astype(np.float32).astype(dtype).astype(np.float64)
    return np.moveaxis((codes * scale).reshape(v.shape), -1, axis)


WIDE = False


def mx_kscale(k):
    if not WIDE:
        return np.ones(k)
    levels = np.array([10, -10, 5, -5, 0])
    if k % 512:
        return np.exp2(np.random.permutation(np.resize(levels, k // 32))).repeat(32)
    a = np.empty((k // 512, 16))
    for p in range(k // 512):
        a[p, :8] = np.random.permutation(np.resize(levels, 8))
        for g in range(8):
            far = levels[np.abs(levels - a[p, g]) >= 10]
            a[p, g + 8] = far[np.random.randint(len(far))]
    return np.exp2(a.ravel()).repeat(32)


BF16 = ml_dtypes.bfloat16


def bf(x):
    return np.asarray(x, np.float32).astype(BF16)


def f64(x):
    return np.asarray(x).astype(np.float64)


E2M1 = np.array([0.0, 0.5, 1.0, 1.5, 2.0, 3.0, 4.0, 6.0, -0.0, -0.5, -1.0, -1.5, -2.0, -3.0, -4.0, -6.0])


def pack_weight(w, fmt):
    k, n = w.shape
    w = f64(bf(w)).reshape(k // 32, 32, n)
    amax = np.abs(w).max(1)
    if fmt == "e4m3":
        byte = np.frexp(amax)[1] - 1 + 127 - 7
    else:
        mant, ex = np.frexp(amax / 6.0)
        byte = np.where(mant > 0.5, ex, ex - 1) + 127
    byte = np.clip(np.where(amax > 0, byte, 1), 1, 254)
    scaled = (w * np.exp2(127.0 - byte)[:, None, :]).reshape(k, n).astype(np.float32)
    by_word = np.ascontiguousarray(scaled.reshape(k // 512, 128, 4, n).transpose(0, 1, 3, 2))
    if fmt == "e4m3":
        words = by_word.astype(ml_dtypes.float8_e4m3fn).view(np.uint8)
    else:
        c = by_word.astype(ml_dtypes.float4_e2m1fn).view(np.uint8) & 0xF
        words = c[..., 0::2] | (c[..., 1::2] << 4)
    return np.ascontiguousarray(words), np.ascontiguousarray(byte.astype(np.uint8).reshape(k // 512, 16, n))


def unpack_weight(words, scales, fmt):
    g, p, n, _ = words.shape
    if fmt == "e4m3":
        vals = np.ascontiguousarray(words).view(ml_dtypes.float8_e4m3fn).astype(np.float64)
    else:
        nib = np.empty((g, p, n, 4), np.uint8)
        nib[..., 0::2] = words & 0xF
        nib[..., 1::2] = words >> 4
        vals = E2M1[nib]
    vals = vals * np.repeat(np.exp2(scales.astype(np.float64) - 127.0), 8, axis=1)[..., None]
    return vals.transpose(0, 1, 3, 2).reshape(g * 512, n)


B, N, C, D = 2, 128, 2048, 2048
ETA, TAU = 1.0, 1.5
FMT = "e4m3"


def setup_inputs():
    s, t = mx_kscale(C), mx_kscale(D)
    a = 2.0 * (C / D) ** 0.25 / np.sqrt(C)
    H_t = bf(np.random.standard_normal((B, N, C)) * s)
    A_stat = bf(np.random.random((N, N)))
    M_mask = bf(np.random.random((N, N)) - 0.25)
    Wq = np.random.standard_normal((D, C)) * a * t[:, None] / s
    Wk = np.random.standard_normal((D, C)) * a / t[:, None] / s
    Wq_words, Wq_scales = pack_weight(np.ascontiguousarray(Wq.T), FMT)
    Wk_words, Wk_scales = pack_weight(np.ascontiguousarray(Wk.T), FMT)
    return {"H_t": H_t,
            "A_stat": A_stat,
            "M_mask": M_mask,
            "Wq_words": Wq_words,
            "Wq_scales": Wq_scales,
            "Wk_words": Wk_words,
            "Wk_scales": Wk_scales}


def reference(H_t, A_stat, M_mask, Wq_words, Wq_scales, Wk_words, Wk_scales):
    c = H_t.shape[-1]
    hq = mxq(f64(H_t), 2, "e4m3")
    Q = hq @ unpack_weight(Wq_words, Wq_scales, FMT)
    K = hq @ unpack_weight(Wk_words, Wk_scales, FMT)
    logits = (mxq(Q, 2, "e4m3") @ mxq(K, 2, "e4m3").transpose(0, 2, 1)) / (np.sqrt(c) * TAU)
    logits = 0.5 * (logits + logits.transpose(0, 2, 1))
    n = logits.shape[-1]
    eye = np.eye(n, dtype=bool)
    logits = np.where(eye[None, :, :], -np.inf, logits)
    A_bias = np.where(eye, 0.0, f64(A_stat))
    logits = logits + ETA * A_bias[None, :, :]
    logits = np.where((f64(M_mask) <= 0)[None, :, :], -np.inf, logits)
    e = np.exp(logits - logits.max(-1, keepdims=True))
    return e / e.sum(-1, keepdims=True)

@@ -1,0 +1,320 @@
+from contextlib import ExitStack
+import math
+
+import concourse.mybir as mybir
+from concourse.masks import make_identity
+
+F32 = mybir.dt.float32
+BF16 = mybir.dt.bfloat16
+I32 = mybir.dt.int32
+U32 = mybir.dt.uint32
+U8 = mybir.dt.uint8
+FP8X4 = mybir.dt.float8_e4m3fn_x4
+ALU = mybir.AluOpType
+ACT = mybir.ActivationFunctionType
+
+P = 128
+B = 2
+C = 2048
+D = 2048
+TOK = B * P
+KG = C // 512
+DG = D // 512
+NCH = 2 * DG
+TAU = 1.5
+BIG = 1.0e30
+SETS = ((0, 0, 2, 4), (0, 2, 2, 0), (1, 0, 2, 4), (1, 2, 1, 0))
+LAST = (1, 3, 1, 2)
+SCALE_RUNS = ((0, 0, 2), (0, 2, 2), (1, 0, 4))
+
+FLOPS = 2 * 2 * B * P * C * D + 2 * B * P * P * D
+
+
+def tile_dynamicgraphattention_w_kernel(
+    tc, H_t, A_stat, M_mask, Wq_words, Wq_scales, Wk_words, Wk_scales, out
+):
+    nc = tc.nc
+    words = (Wq_words, Wk_words)
+    scales = (Wq_scales, Wk_scales)
+    with ExitStack() as ctx:
+        keep = ctx.enter_context(tc.tile_pool(name="keep", bufs=1))
+        ring = ctx.enter_context(tc.tile_pool(name="ring", bufs=4))
+        banks = ctx.enter_context(tc.psum_pool(name="banks", bufs=1))
+        ctx.enter_context(tc.manual_schedule())
+
+        raw_scale = keep.tile([P, 2 * D], U8, align_bytes=64, name="raw_scale")
+        planes = {
+            (x, first): keep.tile([P, 4, n, P], U8, align_bytes=64, name="planes%d_%d" % (x, first))
+            for x, first, n in SCALE_RUNS
+        }
+        h_sb = [keep.tile([P, B, C // 2], BF16, name="h_sb%d" % s) for s in range(2)]
+        raw = {}
+        w_sb = {}
+        zeros = keep.tile([P, 512], BF16, name="zeros")
+        a_bf = keep.tile([P, P], BF16, name="a_bf")
+        m_bf = keep.tile([P, P], BF16, name="m_bf")
+        ident = keep.tile([P, P], F32, name="ident")
+        warm = keep.tile([P, 1], F32, name="warm")
+        warm2 = keep.tile([P, 1], F32, name="warm2")
+
+        nc.vector.memset(ident[:], 0.0)
+        nc.vector.memset(raw_scale[:].bitcast(I32), 0)
+        nc.vector.memset(zeros[:].bitcast(I32), 0)
+        nc.vector.memset(warm[:], 0.0)
+        make_identity(nc, ident[:], nomemset=True)
+
+        def load_scales(queue, x, first, n):
+            lo, hi = 512 * first, 512 * (first + n)
+            for q in range(4):
+                queue.dma_start(
+                    out=raw_scale[32 * q : 32 * q + 16, D * x + lo : D * x + hi].bitcast(F32),
+                    in_=scales[x][:, 4 * q : 4 * q + 4, lo:hi].bitcast(F32),
+                )
+
+        def sort_scales(x, first, n):
+            lo, hi = D * x + 512 * first, D * x + 512 * (first + n)
+            nc.vector.tensor_copy(
+                out=planes[(x, first)][:].rearrange("p t c m -> p (t c m)").bitcast(I32).rearrange(
+                    "p (t q h) -> p t q h", t=4, h=2
+                ),
+                in_=raw_scale[:, lo:hi].bitcast(I32).rearrange("p (q t h) -> p t q h", t=4, h=2),
+            )
+
+        def load_words(x, g, first, n):
+            src = words[x].rearrange("g p n t -> p g (n t)")
+            piece = keep.tile([P, 512 * n], U32, align_bytes=64, name="raw%d_%d_%d" % (x, g, first))
+            nc.sync.dma_start(
+                out=piece[:].bitcast(I32), in_=src[:, g, 2048 * first : 2048 * (first + n)].bitcast(I32)
+            )
+            raw[(x, g, first)] = piece
+
+        def sort_words(x, g, first, n):
+            piece = keep.tile([P, 4, n, P], U32, align_bytes=64, name="w_sb%d_%d_%d" % (x, g, first))
+            nc.vector.tensor_copy(
+                out=piece[:].rearrange("p t c m -> p (t c m)").bitcast(I32).rearrange("p (t q r) -> p t q r", t=4, r=8),
+                in_=raw[(x, g, first)][:].bitcast(I32).rearrange("p (q t r) -> p t q r", t=4, r=8),
+            )
+            for c in range(n):
+                for t in range(4):
+                    w_sb[(x, g, first + c, t)] = piece[:, t, c, :]
+
+        h_src = H_t.rearrange("b n c -> n b c")
+        for s in range(2):
+            nc.sync.dma_start(out=h_sb[s][:], in_=h_src[:, :, (C // 2) * s : (C // 2) * (s + 1)])
+        load_scales(nc.scalar, *SCALE_RUNS[0])
+        nc.scalar.activation(out=warm2[:], in_=warm[:], func=ACT.Exp)
+        for run in SCALE_RUNS[1:]:
+            load_scales(nc.gpsimd, *run)
+        nc.gpsimd.dma_start(out=a_bf[:], in_=A_stat)
+        nc.gpsimd.dma_start(out=m_bf[:], in_=M_mask)
+        for x, first, n, bank in SETS + (LAST,):
+            for g in range(KG):
+                load_words(x, g, first, n)
+
+        idle = banks.tile([P, 512], F32, tag="bank7", name="idle")
+
+        def spin(n):
+            for i in range(n):
+                nc.tensor.matmul(out=idle[:], lhsT=zeros[:, 0:P], rhs=zeros[:], start=True, stop=True)
+
+        spin(6)
+
+        h_words = keep.tile([P, KG, TOK], U32, align_bytes=64, name="h_words")
+        h_scale = keep.tile([P, KG, TOK], U8, align_bytes=64, name="h_scale")
+        h_grp = [keep.tile([P, 4 * TOK], BF16, align_bytes=64, name="h_grp%d" % g) for g in range(KG)]
+        xt = [banks.tile([P, 2, TOK], F32, tag="bank%d" % g, name="xt%d" % g) for g in range(KG)]
+
+        def h_transposes(g):
+            for b in range(B):
+                hw32 = h_sb[g // 2][:, b, :].bitcast(F32)
+                for u in range(2):
+                    nc.tensor.transpose(
+                        xt[g][:, u, P * b : P * (b + 1)],
+                        hw32[:, 256 * (g % 2) + u : 256 * (g % 2 + 1) : 2],
+                        ident[:],
+                    )
+
+        def h_copy(g):
+            dst = h_grp[g][:].bitcast(F32).rearrange("p (w u) -> p w u", u=2)
+            src = xt[g][:].rearrange("p u w -> p w u")
+            if g % 2 == 0:
+                nc.vector.tensor_copy(out=dst, in_=src)
+            else:
+                nc.scalar.copy(out=dst, in_=src)
+
+        def h_quantise(g):
+            nc.vector.quantize_mx(
+                out=h_words[:, g, :].bitcast(FP8X4), scales=h_scale[:, g, :], in_=h_grp[g][:]
+            )
+
+        h_transposes(0)
+        h_transposes(1)
+        spin(1)
+        h_transposes(2)
+        h_transposes(3)
+        h_copy(0)
+        h_copy(1)
+        h_quantise(0)
+        h_copy(2)
+        h_copy(3)
+        h_quantise(1)
+        sort_scales(*SCALE_RUNS[0])
+        sort_words(0, 0, 0, 2)
+        h_quantise(2)
+        sort_words(0, 1, 0, 2)
+        h_quantise(3)
+
+        x_words = [keep.tile([P, TOK], U32, align_bytes=64, name="x_words%d" % c) for c in range(NCH)]
+        x_scale = [keep.tile([P, TOK], U8, align_bytes=64, name="x_scale%d" % c) for c in range(NCH)]
+
+        def plane(x, g, c, t):
+            for sx, first, n in SCALE_RUNS:
+                if sx == x and first <= c < first + n:
+                    return planes[(x, first)][4 * g : P, t, c - first, :]
+
+        def one_pass(dst, x, c, t, g, tok, start, stop):
+            nc.tensor.matmul_mx(
+                out=dst,
+                lhsT=w_sb[(x, g, c, t)].bitcast(FP8X4),
+                lhsT_scale=plane(x, g, c, t),
+                rhs=h_words[:, g, tok].bitcast(FP8X4),
+                rhs_scale=h_scale[:, g, tok],
+                start=start,
+                stop=stop,
+            )
+
+        sums = {}
+
+        def open_banks(x, first, n, bank):
+            for c in range(n):
+                for u in range(2):
+                    sums[(x, first + c, u)] = banks.tile(
+                        [P, 2, TOK], F32, tag="bank%d" % (bank + 2 * c + u), name="ps%d_%d_%d" % (x, first + c, u)
+                    )
+
+        def passes(x, first, n, g):
+            for c in range(first, first + n):
+                for t in range(4):
+                    one_pass(
+                        sums[(x, c, t // 2)][:, t % 2, :], x, c, t, g, slice(0, TOK),
+                        g == 0 and t % 2 == 0, g == KG - 1 and t % 2 == 1,
+                    )
+
+        grouped = {}
+
+        def copy_chunk(x, c):
+            grouped[(x, c)] = ring.tile([P, 4 * TOK], BF16, align_bytes=64, tag="grouped", name="grouped%d_%d" % (x, c))
+            gview = grouped[(x, c)][:].rearrange("p (w t) -> p w t", t=4)
+            for u in range(2):
+                nc.scalar.copy(
+                    out=gview[:, :, 2 * u : 2 * u + 2], in_=sums[(x, c, u)][:].rearrange("p e w -> p w e")
+                )
+
+        def quantise_chunk(x, c):
+            nc.vector.quantize_mx(
+                out=x_words[DG * x + c][:].bitcast(FP8X4), scales=x_scale[DG * x + c][:], in_=grouped[(x, c)][:]
+            )
+
+        not_i = keep.tile([P, P], F32, name="not_i")
+        allowed = keep.tile([P, P], F32, name="allowed")
+        a_keep = keep.tile([P, P], F32, name="a_keep")
+        neg_b = keep.tile([P, P], F32, name="neg_b")
+
+        def build_mask():
+            nc.vector.tensor_scalar(out=not_i[:], in0=ident[:], scalar1=-1.0, scalar2=1.0, op0=ALU.mult, op1=ALU.add)
+            nc.vector.scalar_tensor_tensor(
+                out=allowed[:], in0=m_bf[:], scalar=0.0, in1=not_i[:], op0=ALU.is_gt, op1=ALU.mult
+            )
+            nc.vector.tensor_tensor(out=a_keep[:], in0=a_bf[:], in1=allowed[:], op=ALU.mult)
+            nc.vector.tensor_scalar(out=neg_b[:], in0=allowed[:], scalar1=-BIG, scalar2=BIG, op0=ALU.mult, op1=ALU.add)
+            nc.vector.tensor_tensor(out=neg_b[:], in0=neg_b[:], in1=a_keep[:], op=ALU.subtract)
+
+        def scores(lg, grp):
+            cq, ck = grp, DG + grp
+            for b in range(B):
+                cols = slice(P * b, P * (b + 1))
+                for second, (l, r) in enumerate(((cq, ck), (ck, cq))):
+                    nc.tensor.matmul_mx(
+                        out=lg[b][:],
+                        lhsT=x_words[l][:, cols].bitcast(FP8X4),
+                        lhsT_scale=x_scale[l][:, cols],
+                        rhs=x_words[r][:, cols].bitcast(FP8X4),
+                        rhs_scale=x_scale[r][:, cols],
+                        start=(grp == 0 and second == 0),
+                        stop=(grp == DG - 1 and second == 1),
+                    )
+
+        waiting = []
+        for i, (x, first, n, bank) in enumerate(SETS):
+            open_banks(x, first, n, bank)
+            for xc in waiting:
+                copy_chunk(*xc)
+            for g in range(KG):
+                if i > 0 or g > 1:
+                    sort_words(x, g, first, n)
+                passes(x, first, n, g)
+                if g > 0 and waiting:
+                    quantise_chunk(*waiting.pop(0))
+                if i == 0 and g == KG - 1:
+                    sort_scales(*SCALE_RUNS[1])
+                    sort_scales(*SCALE_RUNS[2])
+                if i == 1 and g == KG - 1:
+                    build_mask()
+            waiting = [(x, first + c) for c in range(n)]
+
+        x, c = LAST[0], LAST[1]
+        for xc in waiting:
+            copy_chunk(*xc)
+        pl = [banks.tile([P, 4, P], F32, tag="bank%d" % (LAST[3] + b), name="pl%d" % b) for b in range(B)]
+        glast = [keep.tile([P, 4 * P], BF16, align_bytes=64, name="glast%d" % b) for b in range(B)]
+        for g in range(KG):
+            sort_words(x, g, c, 1)
+            if g == 1:
+                for xc in waiting:
+                    quantise_chunk(*xc)
+            if g == KG - 1:
+                lg = [banks.tile([P, P], F32, tag="bank%d" % (4 + b), name="lg%d" % b) for b in range(B)]
+                for grp in range(DG - 1):
+                    scores(lg, grp)
+            for t in range(4):
+                for b in range(B):
+                    one_pass(
+                        pl[b][:, t, :], x, c, t, g, slice(P * b, P * (b + 1)),
+                        g == 0 and t == 0, g == KG - 1 and t == 3,
+                    )
+        for b in range(B):
+            dst = glast[b][:].rearrange("p (w t) -> p w t", t=4)
+            src = pl[b][:].rearrange("p t w -> p w t")
+            if b == 0:
+                nc.scalar.copy(out=dst, in_=src)
+            else:
+                nc.vector.tensor_copy(out=dst, in_=src)
+        for b in range(B):
+            cols = slice(P * b, P * (b + 1))
+            nc.vector.quantize_mx(
+                out=x_words[DG * x + c][:, cols].bitcast(FP8X4), scales=x_scale[DG * x + c][:, cols], in_=glast[b][:]
+            )
+        scores(lg, DG - 1)
+
+        y = keep.tile([P, B, P], F32, name="y")
+        ex = keep.tile([P, B, P], F32, name="ex")
+        res = keep.tile([P, B, P], F32, name="res")
+        nmax = keep.tile([P, B], F32, name="nmax")
+        ssum = keep.tile([P, B], F32, name="ssum")
+        rsum = keep.tile([P, B], F32, name="rsum")
+        cneg = -0.5 / (math.sqrt(C) * TAU)
+        for b in range(B):
+            nc.vector.scalar_tensor_tensor(
+                out=y[:, b, :], in0=lg[b][:], scalar=cneg, in1=neg_b[:], op0=ALU.mult, op1=ALU.add
+            )
+            nc.vector.tensor_reduce(out=nmax[:, b : b + 1], in_=y[:, b, :], axis=mybir.AxisListType.X, op=ALU.min)
+            nc.scalar.activation(
+                out=ex[:, b, :], in_=y[:, b, :], func=ACT.Exp, bias=nmax[:, b : b + 1], scale=-1.0,
+                accum_out=ssum[:, b : b + 1],
+            )
+        for b in range(B):
+            nc.vector.reciprocal(out=rsum[:, b : b + 1], in_=ssum[:, b : b + 1])
+            nc.vector.tensor_scalar(
+                out=res[:, b, :], in0=ex[:, b, :], scalar1=rsum[:, b : b + 1], scalar2=None, op0=ALU.mult
+            )
+            nc.sync.dma_start(out=out[b], in_=res[:, b, :])

@@ -102,9 +102,9 @@ def tile_dynamicgraphattention_w_kernel(
         for s in range(2):
             nc.sync.dma_start(out=h_sb[s][:], in_=h_src[:, :, (C // 2) * s : (C // 2) * (s + 1)])
         load_scales(nc.scalar, *SCALE_RUNS[0])
+        load_scales(nc.scalar, *SCALE_RUNS[1])
         nc.scalar.activation(out=warm2[:], in_=warm[:], func=ACT.Exp)
-        for run in SCALE_RUNS[1:]:
-            load_scales(nc.gpsimd, *run)
+        load_scales(nc.gpsimd, *SCALE_RUNS[2])
         nc.gpsimd.dma_start(out=a_bf[:], in_=A_stat)
         nc.gpsimd.dma_start(out=m_bf[:], in_=M_mask)
         for x, first, n, bank in SETS + (LAST,):
@@ -154,15 +154,17 @@ def tile_dynamicgraphattention_w_kernel(
         h_transposes(3)
         h_copy(0)
         h_copy(1)
+        sort_scales(*SCALE_RUNS[0])
         h_quantise(0)
+        sort_words(0, 0, 0, 2)
         h_copy(2)
         h_copy(3)
         h_quantise(1)
-        sort_scales(*SCALE_RUNS[0])
-        sort_words(0, 0, 0, 2)
-        h_quantise(2)
         sort_words(0, 1, 0, 2)
+        h_quantise(2)
+        sort_words(0, 2, 0, 2)
         h_quantise(3)
+        sort_words(0, 3, 0, 2)
 
         x_words = [keep.tile([P, TOK], U32, align_bytes=64, name="x_words%d" % c) for c in range(NCH)]
         x_scale = [keep.tile([P, TOK], U8, align_bytes=64, name="x_scale%d" % c) for c in range(NCH)]
@@ -244,34 +246,49 @@ def tile_dynamicgraphattention_w_kernel(
                         stop=(grp == DG - 1 and second == 1),
                     )
 
-        waiting = []
-        for i, (x, first, n, bank) in enumerate(SETS):
+        def sort_set(x, first, n, groups):
+            for g in groups:
+                sort_words(x, g, first, n)
+
+        def project(x, first, n, bank):
             open_banks(x, first, n, bank)
-            for xc in waiting:
-                copy_chunk(*xc)
             for g in range(KG):
-                if i > 0 or g > 1:
-                    sort_words(x, g, first, n)
                 passes(x, first, n, g)
-                if g > 0 and waiting:
-                    quantise_chunk(*waiting.pop(0))
-                if i == 0 and g == KG - 1:
-                    sort_scales(*SCALE_RUNS[1])
-                    sort_scales(*SCALE_RUNS[2])
-                if i == 1 and g == KG - 1:
-                    build_mask()
-            waiting = [(x, first + c) for c in range(n)]
+
+        s0, s1, s2, s3 = SETS
+        project(*s0)
+        sort_scales(*SCALE_RUNS[1])
+        sort_set(*s1[:3], range(KG))
+        project(*s1)
+        copy_chunk(0, 0)
+        copy_chunk(0, 1)
+        sort_scales(*SCALE_RUNS[2])
+        sort_set(*s2[:3], (0,))
+        quantise_chunk(0, 0)
+        sort_set(*s2[:3], (1,))
+        quantise_chunk(0, 1)
+        sort_set(*s2[:3], (2, 3))
+        project(*s2)
+        copy_chunk(0, 2)
+        copy_chunk(0, 3)
+        sort_set(*s3[:3], range(KG))
+        quantise_chunk(0, 2)
+        project(*s3)
+        copy_chunk(1, 0)
+        copy_chunk(1, 1)
+        sort_set(*LAST[:3], (0,))
+        quantise_chunk(0, 3)
+        sort_set(*LAST[:3], (1, 2, 3))
+        build_mask()
+        quantise_chunk(1, 0)
+        quantise_chunk(1, 1)
+        copy_chunk(1, 2)
+        quantise_chunk(1, 2)
 
         x, c = LAST[0], LAST[1]
-        for xc in waiting:
-            copy_chunk(*xc)
         pl = [banks.tile([P, 4, P], F32, tag="bank%d" % (LAST[3] + b), name="pl%d" % b) for b in range(B)]
         glast = [keep.tile([P, 4 * P], BF16, align_bytes=64, name="glast%d" % b) for b in range(B)]
         for g in range(KG):
-            sort_words(x, g, c, 1)
-            if g == 1:
-                for xc in waiting:
-                    quantise_chunk(*xc)
             if g == KG - 1:
                 lg = [banks.tile([P, P], F32, tag="bank%d" % (4 + b), name="lg%d" % b) for b in range(B)]
                 for grp in range(DG - 1):

@@ -38,7 +38,7 @@ def tile_dynamicgraphattention_w_kernel(
     scales = (Wq_scales, Wk_scales)
     with ExitStack() as ctx:
         keep = ctx.enter_context(tc.tile_pool(name="keep", bufs=1))
-        ring = ctx.enter_context(tc.tile_pool(name="ring", bufs=4))
+        ring = ctx.enter_context(tc.tile_pool(name="ring", bufs=NCH - 1))
         banks = ctx.enter_context(tc.psum_pool(name="banks", bufs=1))
         ctx.enter_context(tc.manual_schedule())
 
@@ -57,18 +57,20 @@ def tile_dynamicgraphattention_w_kernel(
         warm = keep.tile([P, 1], F32, name="warm")
         warm2 = keep.tile([P, 1], F32, name="warm2")
 
-        nc.vector.memset(ident[:], 0.0)
-        nc.vector.memset(raw_scale[:].bitcast(I32), 0)
-        nc.vector.memset(zeros[:].bitcast(I32), 0)
         nc.vector.memset(warm[:], 0.0)
+        nc.vector.memset(raw_scale[:, 0:D].bitcast(I32), 0)
+        nc.vector.memset(ident[:], 0.0)
+        nc.vector.memset(zeros[:].bitcast(I32), 0)
+        nc.vector.memset(raw_scale[:, D : 2 * D].bitcast(I32), 0)
         make_identity(nc, ident[:], nomemset=True)
 
         def load_scales(queue, x, first, n):
             lo, hi = 512 * first, 512 * (first + n)
+            dt = I32 if queue is nc.sync else F32
             for q in range(4):
                 queue.dma_start(
-                    out=raw_scale[32 * q : 32 * q + 16, D * x + lo : D * x + hi].bitcast(F32),
-                    in_=scales[x][:, 4 * q : 4 * q + 4, lo:hi].bitcast(F32),
+                    out=raw_scale[32 * q : 32 * q + 16, D * x + lo : D * x + hi].bitcast(dt),
+                    in_=scales[x][:, 4 * q : 4 * q + 4, lo:hi].bitcast(dt),
                 )
 
         def sort_scales(x, first, n):
@@ -99,17 +101,23 @@ def tile_dynamicgraphattention_w_kernel(
                     w_sb[(x, g, first + c, t)] = piece[:, t, c, :]
 
         h_src = H_t.rearrange("b n c -> n b c")
-        for s in range(2):
+
+        def load_h(s):
             nc.sync.dma_start(out=h_sb[s][:], in_=h_src[:, :, (C // 2) * s : (C // 2) * (s + 1)])
-        load_scales(nc.scalar, *SCALE_RUNS[0])
-        load_scales(nc.scalar, *SCALE_RUNS[1])
+
         nc.scalar.activation(out=warm2[:], in_=warm[:], func=ACT.Exp)
-        load_scales(nc.gpsimd, *SCALE_RUNS[2])
+        load_scales(nc.gpsimd, 1, 0, DG)
         nc.gpsimd.dma_start(out=a_bf[:], in_=A_stat)
         nc.gpsimd.dma_start(out=m_bf[:], in_=M_mask)
+        load_h(0)
+        load_scales(nc.sync, *SCALE_RUNS[0])
         for x, first, n, bank in SETS + (LAST,):
             for g in range(KG):
                 load_words(x, g, first, n)
+                if (x, first, g) == (0, 0, 0):
+                    load_h(1)
+                if (x, first, g) == (0, 0, 1):
+                    load_scales(nc.sync, *SCALE_RUNS[1])
 
         idle = banks.tile([P, 512], F32, tag="bank7", name="idle")
 
@@ -117,7 +125,7 @@ def tile_dynamicgraphattention_w_kernel(
             for i in range(n):
                 nc.tensor.matmul(out=idle[:], lhsT=zeros[:, 0:P], rhs=zeros[:], start=True, stop=True)
 
-        spin(6)
+        spin(3)
 
         h_words = keep.tile([P, KG, TOK], U32, align_bytes=64, name="h_words")
         h_scale = keep.tile([P, KG, TOK], U8, align_bytes=64, name="h_scale")
@@ -146,25 +154,6 @@ def tile_dynamicgraphattention_w_kernel(
             nc.vector.quantize_mx(
                 out=h_words[:, g, :].bitcast(FP8X4), scales=h_scale[:, g, :], in_=h_grp[g][:]
             )
-
-        h_transposes(0)
-        h_transposes(1)
-        spin(1)
-        h_transposes(2)
-        h_transposes(3)
-        h_copy(0)
-        h_copy(1)
-        sort_scales(*SCALE_RUNS[0])
-        h_quantise(0)
-        sort_words(0, 0, 0, 2)
-        h_copy(2)
-        h_copy(3)
-        h_quantise(1)
-        sort_words(0, 1, 0, 2)
-        h_quantise(2)
-        sort_words(0, 2, 0, 2)
-        h_quantise(3)
-        sort_words(0, 3, 0, 2)
 
         x_words = [keep.tile([P, TOK], U32, align_bytes=64, name="x_words%d" % c) for c in range(NCH)]
         x_scale = [keep.tile([P, TOK], U8, align_bytes=64, name="x_scale%d" % c) for c in range(NCH)]
@@ -246,9 +235,8 @@ def tile_dynamicgraphattention_w_kernel(
                         stop=(grp == DG - 1 and second == 1),
                     )
 
-        def sort_set(x, first, n, groups):
-            for g in groups:
-                sort_words(x, g, first, n)
+        def sort_set_group(s, g):
+            sort_words(s[0], g, s[1], s[2])
 
         def project(x, first, n, bank):
             open_banks(x, first, n, bank)
@@ -256,49 +244,80 @@ def tile_dynamicgraphattention_w_kernel(
                 passes(x, first, n, g)
 
         s0, s1, s2, s3 = SETS
-        project(*s0)
-        sort_scales(*SCALE_RUNS[1])
-        sort_set(*s1[:3], range(KG))
-        project(*s1)
+        h_transposes(0)
+        h_transposes(1)
+        spin(3)
+        h_copy(0)
+        h_copy(1)
+        h_quantise(0)
+        sort_scales(*SCALE_RUNS[0])
+        sort_set_group(s0, 0)
+        open_banks(*s0)
+        passes(*s0[:3], 0)
+        h_quantise(1)
+        sort_set_group(s0, 1)
+        h_transposes(2)
+        h_transposes(3)
+        h_copy(2)
+        h_copy(3)
+        passes(*s0[:3], 1)
+        h_quantise(2)
+        sort_set_group(s0, 2)
+        passes(*s0[:3], 2)
+        h_quantise(3)
+        sort_set_group(s0, 3)
+        passes(*s0[:3], 3)
+
         copy_chunk(0, 0)
         copy_chunk(0, 1)
-        sort_scales(*SCALE_RUNS[2])
-        sort_set(*s2[:3], (0,))
-        quantise_chunk(0, 0)
-        sort_set(*s2[:3], (1,))
-        quantise_chunk(0, 1)
-        sort_set(*s2[:3], (2, 3))
-        project(*s2)
+        sort_scales(*SCALE_RUNS[1])
+        for g in range(KG):
+            sort_set_group(s1, g)
+        project(*s1)
+
         copy_chunk(0, 2)
         copy_chunk(0, 3)
-        sort_set(*s3[:3], range(KG))
-        quantise_chunk(0, 2)
-        project(*s3)
+        sort_scales(*SCALE_RUNS[2])
+        sort_set_group(s2, 0)
+        quantise_chunk(0, 0)
+        sort_set_group(s2, 1)
+        quantise_chunk(0, 1)
+        sort_set_group(s2, 2)
+        sort_set_group(s2, 3)
+        build_mask()
+        project(*s2)
+
         copy_chunk(1, 0)
         copy_chunk(1, 1)
-        sort_set(*LAST[:3], (0,))
+        sort_set_group(s3, 0)
+        sort_set_group(s3, 1)
+        quantise_chunk(0, 2)
+        sort_set_group(s3, 2)
+        sort_set_group(s3, 3)
         quantise_chunk(0, 3)
-        sort_set(*LAST[:3], (1, 2, 3))
-        build_mask()
+        project(*s3)
+        sort_set_group(LAST, 0)
+        sort_set_group(LAST, 1)
         quantise_chunk(1, 0)
-        quantise_chunk(1, 1)
         copy_chunk(1, 2)
+        sort_set_group(LAST, 2)
+        sort_set_group(LAST, 3)
+        quantise_chunk(1, 1)
         quantise_chunk(1, 2)
 
         x, c = LAST[0], LAST[1]
         pl = [banks.tile([P, 4, P], F32, tag="bank%d" % (LAST[3] + b), name="pl%d" % b) for b in range(B)]
         glast = [keep.tile([P, 4 * P], BF16, align_bytes=64, name="glast%d" % b) for b in range(B)]
         for g in range(KG):
-            if g == KG - 1:
-                lg = [banks.tile([P, P], F32, tag="bank%d" % (4 + b), name="lg%d" % b) for b in range(B)]
-                for grp in range(DG - 1):
-                    scores(lg, grp)
             for t in range(4):
                 for b in range(B):
                     one_pass(
                         pl[b][:, t, :], x, c, t, g, slice(P * b, P * (b + 1)),
                         g == 0 and t == 0, g == KG - 1 and t == 3,
                     )
+        lg = [banks.tile([P, P], F32, tag="bank%d" % (4 + b), name="lg%d" % b) for b in range(B)]
+        for grp in range(DG - 1):
+            scores(lg, grp)
         for b in range(B):
             dst = glast[b][:].rearrange("p (w t) -> p w t", t=4)
             src = pl[b][:].rearrange("p t w -> p w t")

@@ -20,12 +20,15 @@ D = 2048
 TOK = B * P
 KG = C // 512
 DG = D // 512
-NCH = 2 * DG
+Q, K = 0, 1
 TAU = 1.5
 BIG = 1.0e30
-SETS = ((0, 0, 2, 4), (0, 2, 2, 0), (1, 0, 2, 4), (1, 2, 1, 0))
-LAST = (1, 3, 1, 2)
-SCALE_RUNS = ((0, 0, 2), (0, 2, 2), (1, 0, 4))
+SET_A = ((Q, 0, 1), (Q, 1, 2))
+SET_B = ((Q, 3, 1),)
+SET_C = ((K, 0, 2),)
+SET_D = ((K, 2, 1),)
+LAST = ((K, 3, 1),)
+SCALE_RUNS = ((Q, 0, 3), (Q, 3, 1), (K, 0, 4))
 
 FLOPS = 2 * 2 * B * P * C * D + 2 * B * P * P * D
 
@@ -38,18 +41,14 @@ def tile_dynamicgraphattention_w_kernel(
     scales = (Wq_scales, Wk_scales)
     with ExitStack() as ctx:
         keep = ctx.enter_context(tc.tile_pool(name="keep", bufs=1))
-        ring = ctx.enter_context(tc.tile_pool(name="ring", bufs=NCH - 1))
         banks = ctx.enter_context(tc.psum_pool(name="banks", bufs=1))
         ctx.enter_context(tc.manual_schedule())
 
         raw_scale = keep.tile([P, 2 * D], U8, align_bytes=64, name="raw_scale")
         planes = {
-            (x, first): keep.tile([P, 4, n, P], U8, align_bytes=64, name="planes%d_%d" % (x, first))
-            for x, first, n in SCALE_RUNS
+            run: keep.tile([P, 4, run[2], P], U8, align_bytes=64, name="planes%d_%d" % run[:2]) for run in SCALE_RUNS
         }
         h_sb = [keep.tile([P, B, C // 2], BF16, name="h_sb%d" % s) for s in range(2)]
-        raw = {}
-        w_sb = {}
         zeros = keep.tile([P, 512], BF16, name="zeros")
         a_bf = keep.tile([P, P], BF16, name="a_bf")
         m_bf = keep.tile([P, P], BF16, name="m_bf")
@@ -57,14 +56,15 @@ def tile_dynamicgraphattention_w_kernel(
         warm = keep.tile([P, 1], F32, name="warm")
         warm2 = keep.tile([P, 1], F32, name="warm2")
 
-        nc.vector.memset(warm[:], 0.0)
         nc.vector.memset(raw_scale[:, 0:D].bitcast(I32), 0)
+        nc.vector.memset(warm[:], 0.0)
         nc.vector.memset(ident[:], 0.0)
         nc.vector.memset(zeros[:].bitcast(I32), 0)
         nc.vector.memset(raw_scale[:, D : 2 * D].bitcast(I32), 0)
         make_identity(nc, ident[:], nomemset=True)
 
-        def load_scales(queue, x, first, n):
+        def load_scales(queue, run):
+            x, first, n = run
             lo, hi = 512 * first, 512 * (first + n)
             dt = I32 if queue is nc.sync else F32
             for q in range(4):
@@ -73,51 +73,57 @@ def tile_dynamicgraphattention_w_kernel(
                     in_=scales[x][:, 4 * q : 4 * q + 4, lo:hi].bitcast(dt),
                 )
 
-        def sort_scales(x, first, n):
-            lo, hi = D * x + 512 * first, D * x + 512 * (first + n)
-            nc.vector.tensor_copy(
-                out=planes[(x, first)][:].rearrange("p t c m -> p (t c m)").bitcast(I32).rearrange(
-                    "p (t q h) -> p t q h", t=4, h=2
-                ),
-                in_=raw_scale[:, lo:hi].bitcast(I32).rearrange("p (q t h) -> p t q h", t=4, h=2),
-            )
-
-        def load_words(x, g, first, n):
-            src = words[x].rearrange("g p n t -> p g (n t)")
-            piece = keep.tile([P, 512 * n], U32, align_bytes=64, name="raw%d_%d_%d" % (x, g, first))
-            nc.sync.dma_start(
-                out=piece[:].bitcast(I32), in_=src[:, g, 2048 * first : 2048 * (first + n)].bitcast(I32)
-            )
-            raw[(x, g, first)] = piece
-
-        def sort_words(x, g, first, n):
-            piece = keep.tile([P, 4, n, P], U32, align_bytes=64, name="w_sb%d_%d_%d" % (x, g, first))
-            nc.vector.tensor_copy(
-                out=piece[:].rearrange("p t c m -> p (t c m)").bitcast(I32).rearrange("p (t q r) -> p t q r", t=4, r=8),
-                in_=raw[(x, g, first)][:].bitcast(I32).rearrange("p (q t r) -> p t q r", t=4, r=8),
-            )
-            for c in range(n):
-                for t in range(4):
-                    w_sb[(x, g, first + c, t)] = piece[:, t, c, :]
-
         h_src = H_t.rearrange("b n c -> n b c")
 
         def load_h(s):
             nc.sync.dma_start(out=h_sb[s][:], in_=h_src[:, :, (C // 2) * s : (C // 2) * (s + 1)])
 
+        raw = {}
+
+        def load_words(pieces, g):
+            for x, first, n in pieces:
+                src = words[x].rearrange("g p n t -> p g (n t)")
+                piece = keep.tile([P, 512 * n], U32, align_bytes=64, name="raw%d_%d_%d" % (x, g, first))
+                nc.sync.dma_start(
+                    out=piece[:].bitcast(I32), in_=src[:, g, 2048 * first : 2048 * (first + n)].bitcast(I32)
+                )
+                for c in range(n):
+                    raw[(x, g, first + c)] = piece[:, 512 * c : 512 * (c + 1)]
+
         nc.scalar.activation(out=warm2[:], in_=warm[:], func=ACT.Exp)
-        load_scales(nc.gpsimd, 1, 0, DG)
+        load_scales(nc.gpsimd, SCALE_RUNS[2])
         nc.gpsimd.dma_start(out=a_bf[:], in_=A_stat)
         nc.gpsimd.dma_start(out=m_bf[:], in_=M_mask)
         load_h(0)
-        load_scales(nc.sync, *SCALE_RUNS[0])
-        for x, first, n, bank in SETS + (LAST,):
+        load_h(1)
+        load_scales(nc.sync, SCALE_RUNS[0])
+        for g in range(KG):
+            load_words(SET_A, g)
+            if g == 1:
+                load_scales(nc.sync, SCALE_RUNS[1])
+        for pieces in (SET_B, SET_C, SET_D, LAST):
             for g in range(KG):
-                load_words(x, g, first, n)
-                if (x, first, g) == (0, 0, 0):
-                    load_h(1)
-                if (x, first, g) == (0, 0, 1):
-                    load_scales(nc.sync, *SCALE_RUNS[1])
+                load_words(pieces, g)
+
+        def sort_scales(run):
+            x, first, n = run
+            lo, hi = D * x + 512 * first, D * x + 512 * (first + n)
+            nc.vector.tensor_copy(
+                out=planes[run][:].rearrange("p t c m -> p (t c m)").bitcast(I32).rearrange(
+                    "p (t q h) -> p t q h", t=4, h=2
+                ),
+                in_=raw_scale[:, lo:hi].bitcast(I32).rearrange("p (q t h) -> p t q h", t=4, h=2),
+            )
+
+        w_sb = {}
+
+        def sort_words(x, g, c):
+            dst = keep.tile([P, 4, P], U32, align_bytes=64, name="w_sb%d_%d_%d" % (x, g, c))
+            nc.vector.tensor_copy(
+                out=dst[:].rearrange("p t m -> p (t m)").bitcast(I32).rearrange("p (t q r) -> p t q r", t=4, r=8),
+                in_=raw[(x, g, c)].bitcast(I32).rearrange("p (q t r) -> p t q r", t=4, r=8),
+            )
+            w_sb[(x, g, c)] = dst
 
         idle = banks.tile([P, 512], F32, tag="bank7", name="idle")
 
@@ -125,48 +131,42 @@ def tile_dynamicgraphattention_w_kernel(
             for i in range(n):
                 nc.tensor.matmul(out=idle[:], lhsT=zeros[:, 0:P], rhs=zeros[:], start=True, stop=True)
 
-        spin(3)
-
         h_words = keep.tile([P, KG, TOK], U32, align_bytes=64, name="h_words")
         h_scale = keep.tile([P, KG, TOK], U8, align_bytes=64, name="h_scale")
         h_grp = [keep.tile([P, 4 * TOK], BF16, align_bytes=64, name="h_grp%d" % g) for g in range(KG)]
-        xt = [banks.tile([P, 2, TOK], F32, tag="bank%d" % g, name="xt%d" % g) for g in range(KG)]
 
-        def h_transposes(g):
+        def h_turn(g, copy):
+            xt = banks.tile([P, 2, TOK], F32, tag="bank%d" % (g % 2), name="xt%d" % g)
             for b in range(B):
                 hw32 = h_sb[g // 2][:, b, :].bitcast(F32)
                 for u in range(2):
                     nc.tensor.transpose(
-                        xt[g][:, u, P * b : P * (b + 1)],
-                        hw32[:, 256 * (g % 2) + u : 256 * (g % 2 + 1) : 2],
-                        ident[:],
+                        xt[:, u, P * b : P * (b + 1)], hw32[:, 256 * (g % 2) + u : 256 * (g % 2 + 1) : 2], ident[:]
                     )
-
-        def h_copy(g):
-            dst = h_grp[g][:].bitcast(F32).rearrange("p (w u) -> p w u", u=2)
-            src = xt[g][:].rearrange("p u w -> p w u")
-            if g % 2 == 0:
-                nc.vector.tensor_copy(out=dst, in_=src)
-            else:
-                nc.scalar.copy(out=dst, in_=src)
-
-        def h_quantise(g):
-            nc.vector.quantize_mx(
-                out=h_words[:, g, :].bitcast(FP8X4), scales=h_scale[:, g, :], in_=h_grp[g][:]
+            copy(
+                out=h_grp[g][:].bitcast(F32).rearrange("p (w u) -> p w u", u=2),
+                in_=xt[:].rearrange("p u w -> p w u"),
             )
 
-        x_words = [keep.tile([P, TOK], U32, align_bytes=64, name="x_words%d" % c) for c in range(NCH)]
-        x_scale = [keep.tile([P, TOK], U8, align_bytes=64, name="x_scale%d" % c) for c in range(NCH)]
+        def h_quantise(g):
+            nc.vector.quantize_mx(out=h_words[:, g, :].bitcast(FP8X4), scales=h_scale[:, g, :], in_=h_grp[g][:])
+
+        x_words = {}
+        x_scale = {}
+        for x in (Q, K):
+            for c in range(DG):
+                x_words[(x, c)] = keep.tile([P, TOK], U32, align_bytes=64, name="x_words%d_%d" % (x, c))
+                x_scale[(x, c)] = keep.tile([P, TOK], U8, align_bytes=64, name="x_scale%d_%d" % (x, c))
 
         def plane(x, g, c, t):
-            for sx, first, n in SCALE_RUNS:
-                if sx == x and first <= c < first + n:
-                    return planes[(x, first)][4 * g : P, t, c - first, :]
+            for run in SCALE_RUNS:
+                if run[0] == x and run[1] <= c < run[1] + run[2]:
+                    return planes[run][4 * g : P, t, c - run[1], :]
 
         def one_pass(dst, x, c, t, g, tok, start, stop):
             nc.tensor.matmul_mx(
                 out=dst,
-                lhsT=w_sb[(x, g, c, t)].bitcast(FP8X4),
+                lhsT=w_sb[(x, g, c)][:, t, :].bitcast(FP8X4),
                 lhsT_scale=plane(x, g, c, t),
                 rhs=h_words[:, g, tok].bitcast(FP8X4),
                 rhs_scale=h_scale[:, g, tok],
@@ -176,35 +176,56 @@ def tile_dynamicgraphattention_w_kernel(
 
         sums = {}
 
-        def open_banks(x, first, n, bank):
-            for c in range(n):
-                for u in range(2):
-                    sums[(x, first + c, u)] = banks.tile(
-                        [P, 2, TOK], F32, tag="bank%d" % (bank + 2 * c + u), name="ps%d_%d_%d" % (x, first + c, u)
-                    )
-
-        def passes(x, first, n, g):
-            for c in range(first, first + n):
-                for t in range(4):
-                    one_pass(
-                        sums[(x, c, t // 2)][:, t % 2, :], x, c, t, g, slice(0, TOK),
-                        g == 0 and t % 2 == 0, g == KG - 1 and t % 2 == 1,
-                    )
-
-        grouped = {}
-
-        def copy_chunk(x, c):
-            grouped[(x, c)] = ring.tile([P, 4 * TOK], BF16, align_bytes=64, tag="grouped", name="grouped%d_%d" % (x, c))
-            gview = grouped[(x, c)][:].rearrange("p (w t) -> p w t", t=4)
+        def open_banks(x, c, bank):
             for u in range(2):
-                nc.scalar.copy(
-                    out=gview[:, :, 2 * u : 2 * u + 2], in_=sums[(x, c, u)][:].rearrange("p e w -> p w e")
+                sums[(x, c, u)] = banks.tile([P, 2, TOK], F32, tag="bank%d" % (bank + u), name="ps%d_%d_%d" % (x, c, u))
+
+        def passes(x, c, g):
+            for t in range(4):
+                one_pass(
+                    sums[(x, c, t // 2)][:, t % 2, :], x, c, t, g, slice(0, TOK),
+                    g == 0 and t % 2 == 0, g == KG - 1 and t % 2 == 1,
                 )
 
+        grouped = {}
+        for x in (Q, K):
+            for c in range(DG):
+                grouped[(x, c)] = keep.tile([P, 4 * TOK], BF16, align_bytes=64, name="grouped%d_%d" % (x, c))
+
+        def copy_half(x, c, u, on_vector=False):
+            dst = grouped[(x, c)][:].rearrange("p (w t) -> p w t", t=4)[:, :, 2 * u : 2 * u + 2]
+            src = sums[(x, c, u)][:].rearrange("p e w -> p w e")
+            if on_vector:
+                nc.vector.tensor_copy(out=dst, in_=src)
+            else:
+                nc.scalar.copy(out=dst, in_=src)
+
+        def open_batch_banks(x, c, bank):
+            for b in range(B):
+                sums[(x, c, b)] = banks.tile([P, 4, P], F32, tag="bank%d" % (bank + b), name="pb%d_%d_%d" % (x, c, b))
+
+        def batch_passes(x, c, g):
+            for b in range(B):
+                for t in range(4):
+                    one_pass(
+                        sums[(x, c, b)][:, t, :], x, c, t, g, slice(P * b, P * (b + 1)),
+                        g == 0 and t == 0, g == KG - 1 and t == 3,
+                    )
+
+        def copy_batch(x, c, b, on_vector=False):
+            dst = grouped[(x, c)][:, 4 * P * b : 4 * P * (b + 1)].rearrange("p (w t) -> p w t", t=4)
+            src = sums[(x, c, b)][:].rearrange("p t w -> p w t")
+            if on_vector:
+                nc.vector.tensor_copy(out=dst, in_=src)
+            else:
+                nc.scalar.copy(out=dst, in_=src)
+
+        def copy_chunk(x, c):
+            copy_half(x, c, 0)
+            copy_half(x, c, 1)
+
         def quantise_chunk(x, c):
-            nc.vector.quantize_mx(
-                out=x_words[DG * x + c][:].bitcast(FP8X4), scales=x_scale[DG * x + c][:], in_=grouped[(x, c)][:]
-            )
+            nc.vector.quantize_mx(out=x_words[(x, c)][:].bitcast(FP8X4), scales=x_scale[(x, c)][:], in_=grouped[(x, c)][:])
 
         not_i = keep.tile([P, P], F32, name="not_i")
         allowed = keep.tile([P, P], F32, name="allowed")
@@ -220,117 +241,106 @@ def tile_dynamicgraphattention_w_kernel(
             nc.vector.tensor_scalar(out=neg_b[:], in0=allowed[:], scalar1=-BIG, scalar2=BIG, op0=ALU.mult, op1=ALU.add)
             nc.vector.tensor_tensor(out=neg_b[:], in0=neg_b[:], in1=a_keep[:], op=ALU.subtract)
 
-        def scores(lg, grp):
-            cq, ck = grp, DG + grp
+        spin(4)
+        h_turn(0, nc.vector.tensor_copy)
+        h_turn(1, nc.scalar.copy)
+        spin(1)
+        h_turn(2, nc.scalar.copy)
+        h_turn(3, nc.scalar.copy)
+        h_quantise(0)
+        sort_scales(SCALE_RUNS[0])
+        for c in range(3):
+            open_banks(Q, c, 2 + 2 * c)
+        for g in range(KG):
+            for c in range(3):
+                sort_words(Q, g, c)
+                if c == 0 and g < KG - 1:
+                    h_quantise(g + 1)
+                passes(Q, c, g)
+
+        sort_scales(SCALE_RUNS[1])
+        for g in range(KG):
+            sort_words(Q, g, 3)
+        open_banks(Q, 3, 0)
+        for g in range(KG):
+            passes(Q, 3, g)
+
+        for c in range(3):
+            copy_chunk(Q, c)
+        sort_scales(SCALE_RUNS[2])
+        for c in range(2):
+            sort_words(K, 0, c)
+        quantise_chunk(Q, 0)
+        for c in range(2):
+            sort_words(K, 1, c)
+        quantise_chunk(Q, 1)
+        for c in range(2):
+            sort_words(K, 2, c)
+        quantise_chunk(Q, 2)
+        for c in range(2):
+            sort_words(K, 3, c)
+        build_mask()
+        for c in range(2):
+            open_banks(K, c, 2 + 2 * c)
+        for g in range(KG):
+            for c in range(2):
+                passes(K, c, g)
+
+        copy_chunk(Q, 3)
+        sort_words(K, 0, 2)
+        sort_words(K, 1, 2)
+        quantise_chunk(Q, 3)
+        sort_words(K, 2, 2)
+        sort_words(K, 3, 2)
+        open_batch_banks(K, 2, 6)
+        for g in range(KG):
+            batch_passes(K, 2, g)
+
+        copy_chunk(K, 0)
+        copy_half(K, 1, 0)
+        copy_half(K, 1, 1, on_vector=True)
+        sort_words(K, 0, 3)
+        sort_words(K, 1, 3)
+        sort_words(K, 2, 3)
+        quantise_chunk(K, 0)
+        copy_batch(K, 2, 1, on_vector=True)
+        copy_batch(K, 2, 0)
+        sort_words(K, 3, 3)
+        quantise_chunk(K, 1)
+        quantise_chunk(K, 2)
+
+        open_batch_banks(K, 3, 0)
+        for g in range(KG):
+            batch_passes(K, 3, g)
+
+        lg = [banks.tile([P, P], F32, tag="bank%d" % (4 + b), name="lg%d" % b) for b in range(B)]
+
+        def scores(c):
             for b in range(B):
                 cols = slice(P * b, P * (b + 1))
-                for second, (l, r) in enumerate(((cq, ck), (ck, cq))):
+                for l, r in ((Q, K), (K, Q)):
                     nc.tensor.matmul_mx(
                         out=lg[b][:],
-                        lhsT=x_words[l][:, cols].bitcast(FP8X4),
-                        lhsT_scale=x_scale[l][:, cols],
-                        rhs=x_words[r][:, cols].bitcast(FP8X4),
-                        rhs_scale=x_scale[r][:, cols],
-                        start=(grp == 0 and second == 0),
-                        stop=(grp == DG - 1 and second == 1),
+                        lhsT=x_words[(l, c)][:, cols].bitcast(FP8X4),
+                        lhsT_scale=x_scale[(l, c)][:, cols],
+                        rhs=x_words[(r, c)][:, cols].bitcast(FP8X4),
+                        rhs_scale=x_scale[(r, c)][:, cols],
+                        start=(c == 0 and l == Q),
+                        stop=(c == DG - 1 and l == K),
                     )
 
-        def sort_set_group(s, g):
-            sort_words(s[0], g, s[1], s[2])
-
-        def project(x, first, n, bank):
-            open_banks(x, first, n, bank)
-            for g in range(KG):
-                passes(x, first, n, g)
-
-        s0, s1, s2, s3 = SETS
-        h_transposes(0)
-        h_transposes(1)
-        spin(3)
-        h_copy(0)
-        h_copy(1)
-        h_quantise(0)
-        sort_scales(*SCALE_RUNS[0])
-        sort_set_group(s0, 0)
-        open_banks(*s0)
-        passes(*s0[:3], 0)
-        h_quantise(1)
-        sort_set_group(s0, 1)
-        h_transposes(2)
-        h_transposes(3)
-        h_copy(2)
-        h_copy(3)
-        passes(*s0[:3], 1)
-        h_quantise(2)
-        sort_set_group(s0, 2)
-        passes(*s0[:3], 2)
-        h_quantise(3)
-        sort_set_group(s0, 3)
-        passes(*s0[:3], 3)
-
-        copy_chunk(0, 0)
-        copy_chunk(0, 1)
-        sort_scales(*SCALE_RUNS[1])
-        for g in range(KG):
-            sort_set_group(s1, g)
-        project(*s1)
-
-        copy_chunk(0, 2)
-        copy_chunk(0, 3)
-        sort_scales(*SCALE_RUNS[2])
-        sort_set_group(s2, 0)
-        quantise_chunk(0, 0)
-        sort_set_group(s2, 1)
-        quantise_chunk(0, 1)
-        sort_set_group(s2, 2)
-        sort_set_group(s2, 3)
-        build_mask()
-        project(*s2)
-
-        copy_chunk(1, 0)
-        copy_chunk(1, 1)
-        sort_set_group(s3, 0)
-        sort_set_group(s3, 1)
-        quantise_chunk(0, 2)
-        sort_set_group(s3, 2)
-        sort_set_group(s3, 3)
-        quantise_chunk(0, 3)
-        project(*s3)
-        sort_set_group(LAST, 0)
-        sort_set_group(LAST, 1)
-        quantise_chunk(1, 0)
-        copy_chunk(1, 2)
-        sort_set_group(LAST, 2)
-        sort_set_group(LAST, 3)
-        quantise_chunk(1, 1)
-        quantise_chunk(1, 2)
-
-        x, c = LAST[0], LAST[1]
-        pl = [banks.tile([P, 4, P], F32, tag="bank%d" % (LAST[3] + b), name="pl%d" % b) for b in range(B)]
-        glast = [keep.tile([P, 4 * P], BF16, align_bytes=64, name="glast%d" % b) for b in range(B)]
-        for g in range(KG):
-            for t in range(4):
-                for b in range(B):
-                    one_pass(
-                        pl[b][:, t, :], x, c, t, g, slice(P * b, P * (b + 1)),
-                        g == 0 and t == 0, g == KG - 1 and t == 3,
-                    )
-        lg = [banks.tile([P, P], F32, tag="bank%d" % (4 + b), name="lg%d" % b) for b in range(B)]
-        for grp in range(DG - 1):
-            scores(lg, grp)
-        for b in range(B):
-            dst = glast[b][:].rearrange("p (w t) -> p w t", t=4)
-            src = pl[b][:].rearrange("p t w -> p w t")
-            if b == 0:
-                nc.scalar.copy(out=dst, in_=src)
-            else:
-                nc.vector.tensor_copy(out=dst, in_=src)
+        for c in range(DG - 1):
+            scores(c)
+        copy_batch(K, 3, 0, on_vector=True)
+        copy_batch(K, 3, 1)
         for b in range(B):
             cols = slice(P * b, P * (b + 1))
             nc.vector.quantize_mx(
-                out=x_words[DG * x + c][:, cols].bitcast(FP8X4), scales=x_scale[DG * x + c][:, cols], in_=glast[b][:]
+                out=x_words[(K, 3)][:, cols].bitcast(FP8X4),
+                scales=x_scale[(K, 3)][:, cols],
+                in_=grouped[(K, 3)][:, 4 * P * b : 4 * P * (b + 1)],
             )
-        scores(lg, DG - 1)
+        scores(DG - 1)
 
         y = keep.tile([P, B, P], F32, name="y")
         ex = keep.tile([P, B, P], F32, name="ex")

@@ -28,7 +28,7 @@ SET_B = ((Q, 3, 1),)
 SET_C = ((K, 0, 2),)
 SET_D = ((K, 2, 1),)
 LAST = ((K, 3, 1),)
-SCALE_RUNS = ((Q, 0, 3), (Q, 3, 1), (K, 0, 4))
+SCALE_RUNS = ((Q, 0, 4), (K, 0, 4))
 
 FLOPS = 2 * 2 * B * P * C * D + 2 * B * P * P * D
 
@@ -87,20 +87,21 @@ def tile_dynamicgraphattention_w_kernel(
                 nc.sync.dma_start(
                     out=piece[:].bitcast(I32), in_=src[:, g, 2048 * first : 2048 * (first + n)].bitcast(I32)
                 )
+                raw[(x, g, first, n)] = piece[:]
                 for c in range(n):
-                    raw[(x, g, first + c)] = piece[:, 512 * c : 512 * (c + 1)]
+                    raw[(x, g, first + c, 1)] = piece[:, 512 * c : 512 * (c + 1)]
 
         nc.scalar.activation(out=warm2[:], in_=warm[:], func=ACT.Exp)
-        load_scales(nc.gpsimd, SCALE_RUNS[2])
-        nc.gpsimd.dma_start(out=a_bf[:], in_=A_stat)
-        nc.gpsimd.dma_start(out=m_bf[:], in_=M_mask)
+        load_scales(nc.gpsimd, SCALE_RUNS[1])
         load_h(0)
-        load_h(1)
         load_scales(nc.sync, SCALE_RUNS[0])
-        for g in range(KG):
+        load_words(SET_A[:1], 0)
+        load_h(1)
+        load_words(SET_A[1:], 0)
+        nc.sync.dma_start(out=a_bf[:], in_=A_stat)
+        nc.sync.dma_start(out=m_bf[:], in_=M_mask)
+        for g in range(1, KG):
             load_words(SET_A, g)
-            if g == 1:
-                load_scales(nc.sync, SCALE_RUNS[1])
         for pieces in (SET_B, SET_C, SET_D, LAST):
             for g in range(KG):
                 load_words(pieces, g)
@@ -117,13 +118,14 @@ def tile_dynamicgraphattention_w_kernel(
 
         w_sb = {}
 
-        def sort_words(x, g, c):
-            dst = keep.tile([P, 4, P], U32, align_bytes=64, name="w_sb%d_%d_%d" % (x, g, c))
+        def sort_words(x, g, first, n=1):
+            dst = keep.tile([P, 4, n, P], U32, align_bytes=64, name="w_sb%d_%d_%d" % (x, g, first))
             nc.vector.tensor_copy(
-                out=dst[:].rearrange("p t m -> p (t m)").bitcast(I32).rearrange("p (t q r) -> p t q r", t=4, r=8),
-                in_=raw[(x, g, c)].bitcast(I32).rearrange("p (q t r) -> p t q r", t=4, r=8),
+                out=dst[:].rearrange("p t c m -> p (t c m)").bitcast(I32).rearrange("p (t q r) -> p t q r", t=4, r=8),
+                in_=raw[(x, g, first, n)].bitcast(I32).rearrange("p (q t r) -> p t q r", t=4, r=8),
             )
-            w_sb[(x, g, c)] = dst
+            for c in range(n):
+                w_sb[(x, g, first + c)] = dst[:, :, c, :]
 
         idle = banks.tile([P, 512], F32, tag="bank7", name="idle")
 
@@ -192,14 +194,6 @@ def tile_dynamicgraphattention_w_kernel(
             for c in range(DG):
                 grouped[(x, c)] = keep.tile([P, 4 * TOK], BF16, align_bytes=64, name="grouped%d_%d" % (x, c))
 
-        def copy_half(x, c, u, on_vector=False):
-            dst = grouped[(x, c)][:].rearrange("p (w t) -> p w t", t=4)[:, :, 2 * u : 2 * u + 2]
-            src = sums[(x, c, u)][:].rearrange("p e w -> p w e")
-            if on_vector:
-                nc.vector.tensor_copy(out=dst, in_=src)
-            else:
-                nc.scalar.copy(out=dst, in_=src)
-
         def open_batch_banks(x, c, bank):
             for b in range(B):
                 sums[(x, c, b)] = banks.tile([P, 4, P], F32, tag="bank%d" % (bank + b), name="pb%d_%d_%d" % (x, c, b))
@@ -220,9 +214,13 @@ def tile_dynamicgraphattention_w_kernel(
             else:
                 nc.scalar.copy(out=dst, in_=src)
 
+        def copy_half(copy, x, c, u):
+            dst = grouped[(x, c)][:].rearrange("p (w t) -> p w t", t=4)[:, :, 2 * u : 2 * u + 2]
+            copy(out=dst, in_=sums[(x, c, u)][:].rearrange("p e w -> p w e"))
+
         def copy_chunk(x, c):
-            copy_half(x, c, 0)
-            copy_half(x, c, 1)
+            for u in range(2):
+                copy_half(nc.scalar.copy, x, c, u)
 
         def quantise_chunk(x, c):
             nc.vector.quantize_mx(out=x_words[(x, c)][:].bitcast(FP8X4), scales=x_scale[(x, c)][:], in_=grouped[(x, c)][:])
@@ -232,21 +230,24 @@ def tile_dynamicgraphattention_w_kernel(
         a_keep = keep.tile([P, P], F32, name="a_keep")
         neg_b = keep.tile([P, P], F32, name="neg_b")
 
-        def build_mask():
-            nc.vector.tensor_scalar(out=not_i[:], in0=ident[:], scalar1=-1.0, scalar2=1.0, op0=ALU.mult, op1=ALU.add)
-            nc.vector.scalar_tensor_tensor(
+        mask_steps = [
+            lambda: nc.vector.tensor_scalar(
+                out=not_i[:], in0=ident[:], scalar1=-1.0, scalar2=1.0, op0=ALU.mult, op1=ALU.add
+            ),
+            lambda: nc.vector.scalar_tensor_tensor(
                 out=allowed[:], in0=m_bf[:], scalar=0.0, in1=not_i[:], op0=ALU.is_gt, op1=ALU.mult
-            )
-            nc.vector.tensor_tensor(out=a_keep[:], in0=a_bf[:], in1=allowed[:], op=ALU.mult)
-            nc.vector.tensor_scalar(out=neg_b[:], in0=allowed[:], scalar1=-BIG, scalar2=BIG, op0=ALU.mult, op1=ALU.add)
-            nc.vector.tensor_tensor(out=neg_b[:], in0=neg_b[:], in1=a_keep[:], op=ALU.subtract)
+            ),
+            lambda: nc.vector.tensor_tensor(out=a_keep[:], in0=a_bf[:], in1=allowed[:], op=ALU.mult),
+            lambda: nc.vector.tensor_scalar(
+                out=neg_b[:], in0=allowed[:], scalar1=-BIG, scalar2=BIG, op0=ALU.mult, op1=ALU.add
+            ),
+            lambda: nc.vector.tensor_tensor(out=neg_b[:], in0=neg_b[:], in1=a_keep[:], op=ALU.subtract),
+        ]
 
         spin(4)
         h_turn(0, nc.vector.tensor_copy)
         h_turn(1, nc.scalar.copy)
-        spin(1)
-        h_turn(2, nc.scalar.copy)
-        h_turn(3, nc.scalar.copy)
+        spin(2)
         h_quantise(0)
         sort_scales(SCALE_RUNS[0])
         for c in range(3):
@@ -256,9 +257,13 @@ def tile_dynamicgraphattention_w_kernel(
                 sort_words(Q, g, c)
                 if c == 0 and g < KG - 1:
                     h_quantise(g + 1)
+                if g > 0 and c > 0 and 2 * (g - 1) + c - 1 < len(mask_steps):
+                    mask_steps[2 * (g - 1) + c - 1]()
                 passes(Q, c, g)
+                if (g, c) == (0, 0):
+                    h_turn(2, nc.scalar.copy)
+                    h_turn(3, nc.scalar.copy)
 
-        sort_scales(SCALE_RUNS[1])
         for g in range(KG):
             sort_words(Q, g, 3)
         open_banks(Q, 3, 0)
@@ -267,19 +272,14 @@ def tile_dynamicgraphattention_w_kernel(
 
         for c in range(3):
             copy_chunk(Q, c)
-        sort_scales(SCALE_RUNS[2])
-        for c in range(2):
-            sort_words(K, 0, c)
+        sort_scales(SCALE_RUNS[1])
+        sort_words(K, 0, 0, 2)
         quantise_chunk(Q, 0)
-        for c in range(2):
-            sort_words(K, 1, c)
+        sort_words(K, 1, 0, 2)
         quantise_chunk(Q, 1)
-        for c in range(2):
-            sort_words(K, 2, c)
+        sort_words(K, 2, 0, 2)
         quantise_chunk(Q, 2)
-        for c in range(2):
-            sort_words(K, 3, c)
-        build_mask()
+        sort_words(K, 3, 0, 2)
         for c in range(2):
             open_banks(K, c, 2 + 2 * c)
         for g in range(KG):
@@ -292,20 +292,19 @@ def tile_dynamicgraphattention_w_kernel(
         quantise_chunk(Q, 3)
         sort_words(K, 2, 2)
         sort_words(K, 3, 2)
-        open_batch_banks(K, 2, 6)
+        open_banks(K, 2, 6)
         for g in range(KG):
-            batch_passes(K, 2, g)
+            passes(K, 2, g)
 
         copy_chunk(K, 0)
-        copy_half(K, 1, 0)
-        copy_half(K, 1, 1, on_vector=True)
+        copy_chunk(K, 1)
         sort_words(K, 0, 3)
         sort_words(K, 1, 3)
         sort_words(K, 2, 3)
         quantise_chunk(K, 0)
-        copy_batch(K, 2, 1, on_vector=True)
-        copy_batch(K, 2, 0)
         sort_words(K, 3, 3)
+        copy_half(nc.scalar.copy, K, 2, 0)
+        copy_half(nc.vector.tensor_copy, K, 2, 1)
         quantise_chunk(K, 1)
         quantise_chunk(K, 2)
 

@@ -28,7 +28,8 @@ SET_B = ((Q, 3, 1),)
 SET_C = ((K, 0, 2),)
 SET_D = ((K, 2, 1),)
 LAST = ((K, 3, 1),)
-SCALE_RUNS = ((Q, 0, 4), (K, 0, 4))
+SET_A_WHOLE = ((Q, 0, 3),)
+SCALE_RUNS = ((Q, 0, 1), (Q, 1, 3), (K, 0, 4))
 
 FLOPS = 2 * 2 * B * P * C * D + 2 * B * P * P * D
 
@@ -57,8 +58,8 @@ def tile_dynamicgraphattention_w_kernel(
         warm2 = keep.tile([P, 1], F32, name="warm2")
 
         nc.vector.memset(raw_scale[:, 0:D].bitcast(I32), 0)
-        nc.vector.memset(warm[:], 0.0)
         nc.vector.memset(ident[:], 0.0)
+        nc.vector.memset(warm[:], 0.0)
         nc.vector.memset(zeros[:].bitcast(I32), 0)
         nc.vector.memset(raw_scale[:, D : 2 * D].bitcast(I32), 0)
         make_identity(nc, ident[:], nomemset=True)
@@ -93,15 +94,17 @@ def tile_dynamicgraphattention_w_kernel(
 
         nc.scalar.activation(out=warm2[:], in_=warm[:], func=ACT.Exp)
         load_scales(nc.gpsimd, SCALE_RUNS[1])
+        load_scales(nc.gpsimd, SCALE_RUNS[2])
         load_h(0)
         load_scales(nc.sync, SCALE_RUNS[0])
         load_words(SET_A[:1], 0)
         load_h(1)
         load_words(SET_A[1:], 0)
+        load_words(SET_A_WHOLE, 1)
         nc.sync.dma_start(out=a_bf[:], in_=A_stat)
         nc.sync.dma_start(out=m_bf[:], in_=M_mask)
-        for g in range(1, KG):
-            load_words(SET_A, g)
+        for g in range(2, KG):
+            load_words(SET_A_WHOLE, g)
         for pieces in (SET_B, SET_C, SET_D, LAST):
             for g in range(KG):
                 load_words(pieces, g)
@@ -255,11 +258,16 @@ def tile_dynamicgraphattention_w_kernel(
         for g in range(KG):
             for c in range(3):
                 sort_words(Q, g, c)
+                if (g, c) == (0, 2):
+                    sort_scales(SCALE_RUNS[1])
                 if c == 0 and g < KG - 1:
                     h_quantise(g + 1)
-                if g > 0 and c > 0 and 2 * (g - 1) + c - 1 < len(mask_steps):
-                    mask_steps[2 * (g - 1) + c - 1]()
-                passes(Q, c, g)
+                if g > 1 and 3 * (g - 2) + c < len(mask_steps):
+                    mask_steps[3 * (g - 2) + c]()
+                if (g, c) == (0, 2):
+                    passes(Q, 1, 0)
+                if (g, c) != (0, 1):
+                    passes(Q, c, g)
                 if (g, c) == (0, 0):
                     h_turn(2, nc.scalar.copy)
                     h_turn(3, nc.scalar.copy)
@@ -272,7 +280,7 @@ def tile_dynamicgraphattention_w_kernel(
 
         for c in range(3):
             copy_chunk(Q, c)
-        sort_scales(SCALE_RUNS[1])
+        sort_scales(SCALE_RUNS[2])
         sort_words(K, 0, 0, 2)
         quantise_chunk(Q, 0)
         sort_words(K, 1, 0, 2)

@@ -29,7 +29,7 @@ SET_C = ((K, 0, 2),)
 SET_D = ((K, 2, 1),)
 LAST = ((K, 3, 1),)
 SET_A_WHOLE = ((Q, 0, 3),)
-SCALE_RUNS = ((Q, 0, 1), (Q, 1, 3), (K, 0, 4))
+SCALE_RUNS = ((Q, 0, 2), (Q, 2, 2), (K, 0, 4))
 
 FLOPS = 2 * 2 * B * P * C * D + 2 * B * P * P * D
 
@@ -257,17 +257,14 @@ def tile_dynamicgraphattention_w_kernel(
             open_banks(Q, c, 2 + 2 * c)
         for g in range(KG):
             for c in range(3):
-                sort_words(Q, g, c)
                 if (g, c) == (0, 2):
                     sort_scales(SCALE_RUNS[1])
+                sort_words(Q, g, c)
                 if c == 0 and g < KG - 1:
                     h_quantise(g + 1)
                 if g > 1 and 3 * (g - 2) + c < len(mask_steps):
                     mask_steps[3 * (g - 2) + c]()
-                if (g, c) == (0, 2):
-                    passes(Q, 1, 0)
-                if (g, c) != (0, 1):
-                    passes(Q, c, g)
+                passes(Q, c, g)
                 if (g, c) == (0, 0):
                     h_turn(2, nc.scalar.copy)
                     h_turn(3, nc.scalar.copy)

from contextlib import ExitStack
import math

import concourse.mybir as mybir
from concourse.masks import make_identity

F32 = mybir.dt.float32
BF16 = mybir.dt.bfloat16
I32 = mybir.dt.int32
U32 = mybir.dt.uint32
U8 = mybir.dt.uint8
FP8X4 = mybir.dt.float8_e4m3fn_x4
ALU = mybir.AluOpType
ACT = mybir.ActivationFunctionType

P = 128
B = 2
C = 2048
D = 2048
TOK = B * P
KG = C // 512
DG = D // 512
Q, K = 0, 1
TAU = 1.5
BIG = 1.0e30
SET_A = ((Q, 0, 1), (Q, 1, 2))
SET_B = ((Q, 3, 1),)
SET_C = ((K, 0, 2),)
SET_D = ((K, 2, 1),)
LAST = ((K, 3, 1),)
SET_A_WHOLE = ((Q, 0, 3),)
SCALE_RUNS = ((Q, 0, 2), (Q, 2, 2), (K, 0, 4))

FLOPS = 2 * 2 * B * P * C * D + 2 * B * P * P * D


def tile_dynamicgraphattention_w_kernel(
    tc, H_t, A_stat, M_mask, Wq_words, Wq_scales, Wk_words, Wk_scales, out
):
    nc = tc.nc
    words = (Wq_words, Wk_words)
    scales = (Wq_scales, Wk_scales)
    with ExitStack() as ctx:
        keep = ctx.enter_context(tc.tile_pool(name="keep", bufs=1))
        banks = ctx.enter_context(tc.psum_pool(name="banks", bufs=1))
        ctx.enter_context(tc.manual_schedule())

        raw_scale = keep.tile([P, 2 * D], U8, align_bytes=64, name="raw_scale")
        planes = {
            run: keep.tile([P, 4, run[2], P], U8, align_bytes=64, name="planes%d_%d" % run[:2]) for run in SCALE_RUNS
        }
        h_sb = [keep.tile([P, B, C // 2], BF16, name="h_sb%d" % s) for s in range(2)]
        zeros = keep.tile([P, 512], BF16, name="zeros")
        a_bf = keep.tile([P, P], BF16, name="a_bf")
        m_bf = keep.tile([P, P], BF16, name="m_bf")
        ident = keep.tile([P, P], F32, name="ident")
        warm = keep.tile([P, 1], F32, name="warm")
        warm2 = keep.tile([P, 1], F32, name="warm2")

        nc.vector.memset(raw_scale[:, 0:D].bitcast(I32), 0)
        nc.vector.memset(ident[:], 0.0)
        nc.vector.memset(warm[:], 0.0)
        nc.vector.memset(zeros[:].bitcast(I32), 0)
        nc.vector.memset(raw_scale[:, D : 2 * D].bitcast(I32), 0)
        make_identity(nc, ident[:], nomemset=True)

        def load_scales(queue, run):
            x, first, n = run
            lo, hi = 512 * first, 512 * (first + n)
            dt = I32 if queue is nc.sync else F32
            for q in range(4):
                queue.dma_start(
                    out=raw_scale[32 * q : 32 * q + 16, D * x + lo : D * x + hi].bitcast(dt),
                    in_=scales[x][:, 4 * q : 4 * q + 4, lo:hi].bitcast(dt),
                )

        h_src = H_t.rearrange("b n c -> n b c")

        def load_h(s):
            nc.sync.dma_start(out=h_sb[s][:], in_=h_src[:, :, (C // 2) * s : (C // 2) * (s + 1)])

        raw = {}

        def load_words(pieces, g):
            for x, first, n in pieces:
                src = words[x].rearrange("g p n t -> p g (n t)")
                piece = keep.tile([P, 512 * n], U32, align_bytes=64, name="raw%d_%d_%d" % (x, g, first))
                nc.sync.dma_start(
                    out=piece[:].bitcast(I32), in_=src[:, g, 2048 * first : 2048 * (first + n)].bitcast(I32)
                )
                raw[(x, g, first, n)] = piece[:]
                for c in range(n):
                    raw[(x, g, first + c, 1)] = piece[:, 512 * c : 512 * (c + 1)]

        nc.scalar.activation(out=warm2[:], in_=warm[:], func=ACT.Exp)
        load_scales(nc.gpsimd, SCALE_RUNS[1])
        load_scales(nc.gpsimd, SCALE_RUNS[2])
        load_h(0)
        load_scales(nc.sync, SCALE_RUNS[0])
        load_words(SET_A[:1], 0)
        load_h(1)
        load_words(SET_A[1:], 0)
        load_words(SET_A_WHOLE, 1)
        nc.sync.dma_start(out=a_bf[:], in_=A_stat)
        nc.sync.dma_start(out=m_bf[:], in_=M_mask)
        for g in range(2, KG):
            load_words(SET_A_WHOLE, g)
        for pieces in (SET_B, SET_C, SET_D, LAST):
            for g in range(KG):
                load_words(pieces, g)

        def sort_scales(run):
            x, first, n = run
            lo, hi = D * x + 512 * first, D * x + 512 * (first + n)
            nc.vector.tensor_copy(
                out=planes[run][:].rearrange("p t c m -> p (t c m)").bitcast(I32).rearrange(
                    "p (t q h) -> p t q h", t=4, h=2
                ),
                in_=raw_scale[:, lo:hi].bitcast(I32).rearrange("p (q t h) -> p t q h", t=4, h=2),
            )

        w_sb = {}

        def sort_words(x, g, first, n=1):
            dst = keep.tile([P, 4, n, P], U32, align_bytes=64, name="w_sb%d_%d_%d" % (x, g, first))
            nc.vector.tensor_copy(
                out=dst[:].rearrange("p t c m -> p (t c m)").bitcast(I32).rearrange("p (t q r) -> p t q r", t=4, r=8),
                in_=raw[(x, g, first, n)].bitcast(I32).rearrange("p (q t r) -> p t q r", t=4, r=8),
            )
            for c in range(n):
                w_sb[(x, g, first + c)] = dst[:, :, c, :]

        idle = banks.tile([P, 512], F32, tag="bank7", name="idle")

        def spin(n):
            for i in range(n):
                nc.tensor.matmul(out=idle[:], lhsT=zeros[:, 0:P], rhs=zeros[:], start=True, stop=True)

        h_words = keep.tile([P, KG, TOK], U32, align_bytes=64, name="h_words")
        h_scale = keep.tile([P, KG, TOK], U8, align_bytes=64, name="h_scale")
        h_grp = [keep.tile([P, 4 * TOK], BF16, align_bytes=64, name="h_grp%d" % g) for g in range(KG)]

        def h_turn(g, copy):
            xt = banks.tile([P, 2, TOK], F32, tag="bank%d" % (g % 2), name="xt%d" % g)
            for b in range(B):
                hw32 = h_sb[g // 2][:, b, :].bitcast(F32)
                for u in range(2):
                    nc.tensor.transpose(
                        xt[:, u, P * b : P * (b + 1)], hw32[:, 256 * (g % 2) + u : 256 * (g % 2 + 1) : 2], ident[:]
                    )
            copy(
                out=h_grp[g][:].bitcast(F32).rearrange("p (w u) -> p w u", u=2),
                in_=xt[:].rearrange("p u w -> p w u"),
            )

        def h_quantise(g):
            nc.vector.quantize_mx(out=h_words[:, g, :].bitcast(FP8X4), scales=h_scale[:, g, :], in_=h_grp[g][:])

        x_words = {}
        x_scale = {}
        for x in (Q, K):
            for c in range(DG):
                x_words[(x, c)] = keep.tile([P, TOK], U32, align_bytes=64, name="x_words%d_%d" % (x, c))
                x_scale[(x, c)] = keep.tile([P, TOK], U8, align_bytes=64, name="x_scale%d_%d" % (x, c))

        def plane(x, g, c, t):
            for run in SCALE_RUNS:
                if run[0] == x and run[1] <= c < run[1] + run[2]:
                    return planes[run][4 * g : P, t, c - run[1], :]

        def one_pass(dst, x, c, t, g, tok, start, stop):
            nc.tensor.matmul_mx(
                out=dst,
                lhsT=w_sb[(x, g, c)][:, t, :].bitcast(FP8X4),
                lhsT_scale=plane(x, g, c, t),
                rhs=h_words[:, g, tok].bitcast(FP8X4),
                rhs_scale=h_scale[:, g, tok],
                start=start,
                stop=stop,
            )

        sums = {}

        def open_banks(x, c, bank):
            for u in range(2):
                sums[(x, c, u)] = banks.tile([P, 2, TOK], F32, tag="bank%d" % (bank + u), name="ps%d_%d_%d" % (x, c, u))

        def passes(x, c, g):
            for t in range(4):
                one_pass(
                    sums[(x, c, t // 2)][:, t % 2, :], x, c, t, g, slice(0, TOK),
                    g == 0 and t % 2 == 0, g == KG - 1 and t % 2 == 1,
                )

        grouped = {}
        for x in (Q, K):
            for c in range(DG):
                grouped[(x, c)] = keep.tile([P, 4 * TOK], BF16, align_bytes=64, name="grouped%d_%d" % (x, c))

        def open_batch_banks(x, c, bank):
            for b in range(B):
                sums[(x, c, b)] = banks.tile([P, 4, P], F32, tag="bank%d" % (bank + b), name="pb%d_%d_%d" % (x, c, b))

        def batch_passes(x, c, g):
            for b in range(B):
                for t in range(4):
                    one_pass(
                        sums[(x, c, b)][:, t, :], x, c, t, g, slice(P * b, P * (b + 1)),
                        g == 0 and t == 0, g == KG - 1 and t == 3,
                    )

        def copy_batch(x, c, b, on_vector=False):
            dst = grouped[(x, c)][:, 4 * P * b : 4 * P * (b + 1)].rearrange("p (w t) -> p w t", t=4)
            src = sums[(x, c, b)][:].rearrange("p t w -> p w t")
            if on_vector:
                nc.vector.tensor_copy(out=dst, in_=src)
            else:
                nc.scalar.copy(out=dst, in_=src)

        def copy_half(copy, x, c, u):
            dst = grouped[(x, c)][:].rearrange("p (w t) -> p w t", t=4)[:, :, 2 * u : 2 * u + 2]
            copy(out=dst, in_=sums[(x, c, u)][:].rearrange("p e w -> p w e"))

        def copy_chunk(x, c):
            for u in range(2):
                copy_half(nc.scalar.copy, x, c, u)

        def quantise_chunk(x, c):
            nc.vector.quantize_mx(out=x_words[(x, c)][:].bitcast(FP8X4), scales=x_scale[(x, c)][:], in_=grouped[(x, c)][:])

        not_i = keep.tile([P, P], F32, name="not_i")
        allowed = keep.tile([P, P], F32, name="allowed")
        a_keep = keep.tile([P, P], F32, name="a_keep")
        neg_b = keep.tile([P, P], F32, name="neg_b")

        mask_steps = [
            lambda: nc.vector.tensor_scalar(
                out=not_i[:], in0=ident[:], scalar1=-1.0, scalar2=1.0, op0=ALU.mult, op1=ALU.add
            ),
            lambda: nc.vector.scalar_tensor_tensor(
                out=allowed[:], in0=m_bf[:], scalar=0.0, in1=not_i[:], op0=ALU.is_gt, op1=ALU.mult
            ),
            lambda: nc.vector.tensor_tensor(out=a_keep[:], in0=a_bf[:], in1=allowed[:], op=ALU.mult),
            lambda: nc.vector.tensor_scalar(
                out=neg_b[:], in0=allowed[:], scalar1=-BIG, scalar2=BIG, op0=ALU.mult, op1=ALU.add
            ),
            lambda: nc.vector.tensor_tensor(out=neg_b[:], in0=neg_b[:], in1=a_keep[:], op=ALU.subtract),
        ]

        spin(4)
        h_turn(0, nc.vector.tensor_copy)
        h_turn(1, nc.scalar.copy)
        spin(2)
        h_quantise(0)
        sort_scales(SCALE_RUNS[0])
        for c in range(3):
            open_banks(Q, c, 2 + 2 * c)
        for g in range(KG):
            for c in range(3):
                if (g, c) == (0, 2):
                    sort_scales(SCALE_RUNS[1])
                sort_words(Q, g, c)
                if c == 0 and g < KG - 1:
                    h_quantise(g + 1)
                if g > 1 and 3 * (g - 2) + c < len(mask_steps):
                    mask_steps[3 * (g - 2) + c]()
                passes(Q, c, g)
                if (g, c) == (0, 0):
                    h_turn(2, nc.scalar.copy)
                    h_turn(3, nc.scalar.copy)

        for g in range(KG):
            sort_words(Q, g, 3)
        open_banks(Q, 3, 0)
        for g in range(KG):
            passes(Q, 3, g)

        for c in range(3):
            copy_chunk(Q, c)
        sort_scales(SCALE_RUNS[2])
        sort_words(K, 0, 0, 2)
        quantise_chunk(Q, 0)
        sort_words(K, 1, 0, 2)
        quantise_chunk(Q, 1)
        sort_words(K, 2, 0, 2)
        quantise_chunk(Q, 2)
        sort_words(K, 3, 0, 2)
        for c in range(2):
            open_banks(K, c, 2 + 2 * c)
        for g in range(KG):
            for c in range(2):
                passes(K, c, g)

        copy_chunk(Q, 3)
        sort_words(K, 0, 2)
        sort_words(K, 1, 2)
        quantise_chunk(Q, 3)
        sort_words(K, 2, 2)
        sort_words(K, 3, 2)
        open_banks(K, 2, 6)
        for g in range(KG):
            passes(K, 2, g)

        copy_chunk(K, 0)
        copy_chunk(K, 1)
        sort_words(K, 0, 3)
        sort_words(K, 1, 3)
        sort_words(K, 2, 3)
        quantise_chunk(K, 0)
        sort_words(K, 3, 3)
        copy_half(nc.scalar.copy, K, 2, 0)
        copy_half(nc.vector.tensor_copy, K, 2, 1)
        quantise_chunk(K, 1)
        quantise_chunk(K, 2)

        open_batch_banks(K, 3, 0)
        for g in range(KG):
            batch_passes(K, 3, g)

        lg = [banks.tile([P, P], F32, tag="bank%d" % (4 + b), name="lg%d" % b) for b in range(B)]

        def scores(c):
            for b in range(B):
                cols = slice(P * b, P * (b + 1))
                for l, r in ((Q, K), (K, Q)):
                    nc.tensor.matmul_mx(
                        out=lg[b][:],
                        lhsT=x_words[(l, c)][:, cols].bitcast(FP8X4),
                        lhsT_scale=x_scale[(l, c)][:, cols],
                        rhs=x_words[(r, c)][:, cols].bitcast(FP8X4),
                        rhs_scale=x_scale[(r, c)][:, cols],
                        start=(c == 0 and l == Q),
                        stop=(c == DG - 1 and l == K),
                    )

        for c in range(DG - 1):
            scores(c)
        copy_batch(K, 3, 0, on_vector=True)
        copy_batch(K, 3, 1)
        for b in range(B):
            cols = slice(P * b, P * (b + 1))
            nc.vector.quantize_mx(
                out=x_words[(K, 3)][:, cols].bitcast(FP8X4),
                scales=x_scale[(K, 3)][:, cols],
                in_=grouped[(K, 3)][:, 4 * P * b : 4 * P * (b + 1)],
            )
        scores(DG - 1)

        y = keep.tile([P, B, P], F32, name="y")
        ex = keep.tile([P, B, P], F32, name="ex")
        res = keep.tile([P, B, P], F32, name="res")
        nmax = keep.tile([P, B], F32, name="nmax")
        ssum = keep.tile([P, B], F32, name="ssum")
        rsum = keep.tile([P, B], F32, name="rsum")
        cneg = -0.5 / (math.sqrt(C) * TAU)
        for b in range(B):
            nc.vector.scalar_tensor_tensor(
                out=y[:, b, :], in0=lg[b][:], scalar=cneg, in1=neg_b[:], op0=ALU.mult, op1=ALU.add
            )
            nc.vector.tensor_reduce(out=nmax[:, b : b + 1], in_=y[:, b, :], axis=mybir.AxisListType.X, op=ALU.min)
            nc.scalar.activation(
                out=ex[:, b, :], in_=y[:, b, :], func=ACT.Exp, bias=nmax[:, b : b + 1], scale=-1.0,
                accum_out=ssum[:, b : b + 1],
            )
        for b in range(B):
            nc.vector.reciprocal(out=rsum[:, b : b + 1], in_=ssum[:, b : b + 1])
            nc.vector.tensor_scalar(
                out=res[:, b, :], in0=ex[:, b, :], scalar1=rsum[:, b : b + 1], scalar2=None, op0=ALU.mult
            )
            nc.sync.dma_start(out=out[b], in_=res[:, b, :])
